import numpy as np
import ml_dtypes


def mxq(x, axis, fmt="e4m3"):
    dtype, down = {"e4m3": (ml_dtypes.float8_e4m3fn, 7), "e5m2": (ml_dtypes.float8_e5m2, 14)}[fmt]
    v = np.moveaxis(np.asarray(x, np.float32).astype(ml_dtypes.bfloat16).astype(np.float64), axis, -1)
    blocks = v.reshape(v.shape[:-1] + (-1, 32))
    amax = np.abs(blocks).max(-1, keepdims=True)
    byte = np.maximum(np.where(amax > 0, np.frexp(amax)[1] - 1 + 127, 0) - down, 1)
    scale = np.exp2(byte - 127.0)
    codes = (blocks / scale).astype(np.float32).astype(dtype).astype(np.float64)
    return np.moveaxis((codes * scale).reshape(v.shape), -1, axis)


WIDE = False


def mx_kscale(k):
    if not WIDE:
        return np.ones(k)
    levels = np.array([10, -10, 5, -5, 0])
    a = np.random.permutation(np.resize(levels, k // 512 * 4)).reshape(k // 512, 4)
    idx = np.arange(k)
    return np.exp2(a[idx // 512, idx % 128 // 32])


BF16 = ml_dtypes.bfloat16


def bf(x):
    return np.asarray(x, np.float32).astype(BF16)


def f64(x):
    return np.asarray(x).astype(np.float64)


S, D, N_HEADS, N_KV_HEADS, HEAD_DIM = 512, 2048, 16, 4, 128
Q_DIM = N_HEADS * HEAD_DIM
KV_DIM = N_KV_HEADS * HEAD_DIM
ROPE_THETA = 500000.0


def apply_rope(t, cos, sin):
    te = t[:, :, ::2]
    to = t[:, :, 1::2]
    c = cos[:, None, :]
    s = sin[:, None, :]
    te_rot = te * c - to * s
    to_rot = te * s + to * c
    return np.stack([te_rot, to_rot], axis=-1).reshape(t.shape)


def setup_inputs():
    s = mx_kscale(D)
    inv_freq = 1.0 / ROPE_THETA ** (np.arange(0, HEAD_DIM, 2) / HEAD_DIM)
    angles = np.arange(S)[:, None] * inv_freq[None, :]
    return {"x": bf(np.random.standard_normal((S, D)) * s),
            "freqs_cos": bf(np.cos(angles)),
            "freqs_sin": bf(np.sin(angles)),
            "wqkv": bf(np.random.standard_normal((Q_DIM + 2 * KV_DIM, D)) / np.sqrt(D) / s[None, :])}


def reference(x, freqs_cos, freqs_sin, wqkv):
    qkv = mxq(f64(x), 1, "e4m3") @ mxq(f64(wqkv), 1, "e4m3").T
    q = qkv[:, :Q_DIM].reshape(S, N_HEADS, HEAD_DIM)
    k = qkv[:, Q_DIM:Q_DIM + KV_DIM].reshape(S, N_KV_HEADS, HEAD_DIM)
    v = qkv[:, Q_DIM + KV_DIM:].reshape(S, N_KV_HEADS, HEAD_DIM)
    cos, sin = f64(freqs_cos), f64(freqs_sin)
    return apply_rope(q, cos, sin), apply_rope(k, cos, sin), v

@@ -1,0 +1,188 @@
+from contextlib import ExitStack
+
+import concourse.mybir as mybir
+from concourse.masks import make_identity
+
+F32 = mybir.dt.float32
+BF16 = mybir.dt.bfloat16
+U32 = mybir.dt.uint32
+U8 = mybir.dt.uint8
+FP8X4 = mybir.dt.float8_e4m3fn_x4
+MULT = mybir.AluOpType.mult
+ADD = mybir.AluOpType.add
+
+P = 128
+S = 512
+D = 2048
+Q_DIM = 2048
+KV_DIM = 512
+HEAD_DIM = 128
+PAIRS = HEAD_DIM // 2
+
+PACK = 4
+K_PASS = P * PACK
+PASSES = D // K_PASS
+WORD_HALVES = 2
+UNIT = 256
+UNIT_TILES = UNIT // P
+X_UNITS = S // UNIT
+W_UNITS = (Q_DIM + 2 * KV_DIM) // UNIT
+ROTATED_UNITS = (Q_DIM + KV_DIM) // UNIT
+UNIT_HEADS = UNIT // HEAD_DIM
+TOKEN_TILES = S // P
+STORE_UNITS = 2
+STORE_COLS = STORE_UNITS * UNIT
+LOADS_AHEAD = 6
+
+FLOPS = 2 * S * (Q_DIM + 2 * KV_DIM) * D
+
+assert KV_DIM == STORE_COLS
+
+
+def tile_mha_pa_kernel(tc, x, freqs_cos, freqs_sin, wqkv, out_0, out_1, out_2):
+    nc = tc.nc
+
+    x_units = x.rearrange("(p n j) k -> n p j k", n=X_UNITS, j=UNIT_TILES)
+    cos_rows = freqs_cos.rearrange("(p m) i -> p m i", m=TOKEN_TILES)
+    sin_rows = freqs_sin.rearrange("(p m) i -> p m i", m=TOKEN_TILES)
+    w_units = wqkv.rearrange("(n p j) k -> n p j k", p=P, j=UNIT_TILES)
+    q_rows = out_0.rearrange("(p m) h d -> p m (h d)", m=TOKEN_TILES)
+    k_rows = out_1.rearrange("(p m) h d -> p m (h d)", m=TOKEN_TILES)
+    v_rows = out_2.rearrange("(p m) h d -> p m (h d)", m=TOKEN_TILES)
+    store_targets = [q_rows[:, :, c : c + STORE_COLS] for c in range(0, Q_DIM, STORE_COLS)] + [k_rows, v_rows]
+
+    with ExitStack() as ctx:
+        const = ctx.enter_context(tc.tile_pool(name="const", bufs=1))
+        raw_pool = ctx.enter_context(tc.tile_pool(name="raw", bufs=1))
+        grouped_pool = ctx.enter_context(tc.tile_pool(name="grouped", bufs=3))
+        w_mx_pool = ctx.enter_context(tc.tile_pool(name="w_mx", bufs=3))
+        product_pool = ctx.enter_context(tc.tile_pool(name="product", bufs=4))
+        result_pool = ctx.enter_context(tc.tile_pool(name="result", bufs=3))
+        flipped_pool = ctx.enter_context(tc.psum_pool(name="flipped", bufs=PASSES))
+        acc_pool = ctx.enter_context(tc.psum_pool(name="acc", bufs=2 * X_UNITS))
+        ctx.enter_context(tc.manual_schedule())
+
+        def load_unit(rows, name):
+            raw = raw_pool.tile([P, UNIT_TILES, D], BF16, name=name)
+            nc.sync.dma_start(out=raw[:], in_=rows)
+            return raw
+
+        cos_sb = const.tile([P, TOKEN_TILES, PAIRS], BF16)
+        sin_sb = const.tile([P, TOKEN_TILES, PAIRS], BF16)
+        nc.scalar.dma_start(out=cos_sb[:], in_=cos_rows)
+        nc.scalar.dma_start(out=sin_sb[:], in_=sin_rows)
+        x_raw = [load_unit(x_units[n, :, :, :], "x_raw%d" % n) for n in range(X_UNITS)]
+        w_raw = [load_unit(w_units[n, :, :, :], "w_raw%d" % n) for n in range(LOADS_AHEAD)]
+
+        ident = const.tile([P, P], F32)
+        make_identity(nc, ident[:])
+
+        first_table = const.tile([P, TOKEN_TILES, UNIT_HEADS, PAIRS, 2], F32)
+        second_table = const.tile([P, TOKEN_TILES, UNIT_HEADS, PAIRS, 2], F32)
+        over_heads = [P, TOKEN_TILES, UNIT_HEADS, PAIRS]
+        cos_heads = cos_sb[:].unsqueeze(2).to_broadcast(over_heads)
+        sin_heads = sin_sb[:].unsqueeze(2).to_broadcast(over_heads)
+        nc.vector.tensor_copy(out=first_table[:, :, :, :, 0], in_=cos_heads)
+        nc.vector.tensor_copy(out=first_table[:, :, :, :, 1], in_=sin_heads)
+        nc.vector.tensor_scalar_mul(out=second_table[:, :, :, :, 0], in0=sin_heads, scalar1=-1.0)
+        nc.vector.tensor_copy(out=second_table[:, :, :, :, 1], in_=cos_heads)
+
+        def transpose_unit(raw):
+            grouped = grouped_pool.tile([P, PASSES * UNIT * PACK], BF16, align_bytes=64)
+            grouped_words = grouped[:].bitcast(F32).rearrange(
+                "p (g j r u) -> p g j r u", g=PASSES, j=UNIT_TILES, u=WORD_HALVES
+            )
+            for g in range(PASSES):
+                flipped = flipped_pool.tile([P, UNIT_TILES, WORD_HALVES, P], F32)
+                for j in range(UNIT_TILES):
+                    raw_words = raw[:, j, :].bitcast(F32)
+                    for u in range(WORD_HALVES):
+                        first = (WORD_HALVES * g + u) * P
+                        nc.tensor.transpose(flipped[:, j, u, :], raw_words[:, first : first + P], ident[:])
+                nc.scalar.copy(out=grouped_words[:, g, :, :, :], in_=flipped[:].rearrange("p j u r -> p j r u"))
+            return grouped
+
+        def quantise_unit(grouped, pool, name):
+            codes = pool.tile([P, PASSES, UNIT], U32, name=name + "_codes", align_bytes=64)
+            scales = pool.tile([P, PASSES, UNIT], U8, name=name + "_scales", align_bytes=64)
+            nc.vector.quantize_mx(
+                out=codes[:].rearrange("p g c -> p (g c)").bitcast(FP8X4),
+                scales=scales[:].rearrange("p g c -> p (g c)"),
+                in_=grouped[:],
+            )
+            return codes, scales
+
+        def multiply(x_unit, w_unit):
+            x_codes, x_scales = x_unit
+            w_codes, w_scales = w_unit
+            acc = acc_pool.tile([P, UNIT_TILES, UNIT], F32)
+            for j in range(UNIT_TILES):
+                tokens = slice(j * P, (j + 1) * P)
+                for g in range(PASSES):
+                    nc.tensor.matmul_mx(
+                        out=acc[:, j, :],
+                        lhsT=x_codes[:, g, tokens].bitcast(FP8X4),
+                        lhsT_scale=x_scales[:, g, tokens],
+                        rhs=w_codes[:, g, :].bitcast(FP8X4),
+                        rhs_scale=w_scales[:, g, :],
+                        start=(g == 0),
+                        stop=(g == PASSES - 1),
+                    )
+            return acc
+
+        def rotate(acc, tiles, rotated):
+            pair_shape = [P, UNIT_TILES, P, 2]
+            from_first = product_pool.tile(pair_shape, F32)
+            from_second = product_pool.tile(pair_shape, F32)
+            nc.vector.tensor_tensor(
+                out=from_first[:],
+                in0=acc[:, :, 0:P].unsqueeze(3).to_broadcast(pair_shape),
+                in1=first_table[:, tiles, :, :, :].rearrange("p m h i e -> p m (h i) e"),
+                op=MULT,
+            )
+            nc.vector.tensor_tensor(
+                out=from_second[:],
+                in0=acc[:, :, P:UNIT].unsqueeze(3).to_broadcast(pair_shape),
+                in1=second_table[:, tiles, :, :, :].rearrange("p m h i e -> p m (h i) e"),
+                op=MULT,
+            )
+            nc.gpsimd.tensor_tensor(
+                out=rotated,
+                in0=from_first[:].rearrange("p m r e -> p m (r e)"),
+                in1=from_second[:].rearrange("p m r e -> p m (r e)"),
+                op=ADD,
+            )
+
+        def interleave(acc, plain):
+            nc.scalar.copy(
+                out=plain.rearrange("p m (r j) -> p m r j", j=UNIT_TILES),
+                in_=acc[:].rearrange("p m (j r) -> p m r j", j=UNIT_TILES),
+            )
+
+        x_grouped = [transpose_unit(x_raw[n]) for n in range(X_UNITS)]
+        x_mx = [quantise_unit(x_grouped[n], const, "x%d" % n) for n in range(X_UNITS)]
+        w_mx = quantise_unit(transpose_unit(w_raw[0]), w_mx_pool, "w")
+
+        result = None
+        for n in range(W_UNITS):
+            if n + LOADS_AHEAD < W_UNITS:
+                w_raw.append(load_unit(w_units[n + LOADS_AHEAD, :, :, :], "w_raw%d" % (n + LOADS_AHEAD)))
+            following = n + 1 < W_UNITS
+            if following:
+                w_grouped = transpose_unit(w_raw[n + 1])
+            banks = [multiply(x_mx[b], w_mx) for b in range(X_UNITS)]
+            if following:
+                w_mx = quantise_unit(w_grouped, w_mx_pool, "w")
+
+            part = n % STORE_UNITS
+            if part == 0:
+                result = result_pool.tile([P, TOKEN_TILES, STORE_COLS], F32, name="result")
+            for b in range(X_UNITS):
+                tiles = slice(b * UNIT_TILES, (b + 1) * UNIT_TILES)
+                unit_result = result[:, tiles, part * UNIT : (part + 1) * UNIT]
+                if n < ROTATED_UNITS:
+                    rotate(banks[b], tiles, unit_result)
+                else:
+                    interleave(banks[b], unit_result)
+                if part == STORE_UNITS - 1:
+                    nc.sync.dma_start(out=store_targets[n // STORE_UNITS][:, tiles, :], in_=result[:, tiles, :])

@@ -30,13 +30,9 @@ W_UNITS = (Q_DIM + 2 * KV_DIM) // UNIT
 ROTATED_UNITS = (Q_DIM + KV_DIM) // UNIT
 UNIT_HEADS = UNIT // HEAD_DIM
 TOKEN_TILES = S // P
-STORE_UNITS = 2
-STORE_COLS = STORE_UNITS * UNIT
 LOADS_AHEAD = 6
 
 FLOPS = 2 * S * (Q_DIM + 2 * KV_DIM) * D
-
-assert KV_DIM == STORE_COLS
 
 
 def tile_mha_pa_kernel(tc, x, freqs_cos, freqs_sin, wqkv, out_0, out_1, out_2):
@@ -49,7 +45,11 @@ def tile_mha_pa_kernel(tc, x, freqs_cos, freqs_sin, wqkv, out_0, out_1, out_2):
     q_rows = out_0.rearrange("(p m) h d -> p m (h d)", m=TOKEN_TILES)
     k_rows = out_1.rearrange("(p m) h d -> p m (h d)", m=TOKEN_TILES)
     v_rows = out_2.rearrange("(p m) h d -> p m (h d)", m=TOKEN_TILES)
-    store_targets = [q_rows[:, :, c : c + STORE_COLS] for c in range(0, Q_DIM, STORE_COLS)] + [k_rows, v_rows]
+    unit_targets = [
+        rows[:, :, c : c + UNIT]
+        for rows, width in ((q_rows, Q_DIM), (k_rows, KV_DIM), (v_rows, KV_DIM))
+        for c in range(0, width, UNIT)
+    ]
 
     with ExitStack() as ctx:
         const = ctx.enter_context(tc.tile_pool(name="const", bufs=1))
@@ -57,7 +57,7 @@ def tile_mha_pa_kernel(tc, x, freqs_cos, freqs_sin, wqkv, out_0, out_1, out_2):
         grouped_pool = ctx.enter_context(tc.tile_pool(name="grouped", bufs=3))
         w_mx_pool = ctx.enter_context(tc.tile_pool(name="w_mx", bufs=3))
         product_pool = ctx.enter_context(tc.tile_pool(name="product", bufs=4))
-        result_pool = ctx.enter_context(tc.tile_pool(name="result", bufs=3))
+        result_pool = ctx.enter_context(tc.tile_pool(name="result", bufs=8))
         flipped_pool = ctx.enter_context(tc.psum_pool(name="flipped", bufs=PASSES))
         acc_pool = ctx.enter_context(tc.psum_pool(name="acc", bufs=2 * X_UNITS))
         ctx.enter_context(tc.manual_schedule())
@@ -163,7 +163,6 @@ def tile_mha_pa_kernel(tc, x, freqs_cos, freqs_sin, wqkv, out_0, out_1, out_2):
         x_mx = [quantise_unit(x_grouped[n], const, "x%d" % n) for n in range(X_UNITS)]
         w_mx = quantise_unit(transpose_unit(w_raw[0]), w_mx_pool, "w")
 
-        result = None
         for n in range(W_UNITS):
             if n + LOADS_AHEAD < W_UNITS:
                 w_raw.append(load_unit(w_units[n + LOADS_AHEAD, :, :, :], "w_raw%d" % (n + LOADS_AHEAD)))
@@ -174,15 +173,11 @@ def tile_mha_pa_kernel(tc, x, freqs_cos, freqs_sin, wqkv, out_0, out_1, out_2):
             if following:
                 w_mx = quantise_unit(w_grouped, w_mx_pool, "w")
 
-            part = n % STORE_UNITS
-            if part == 0:
-                result = result_pool.tile([P, TOKEN_TILES, STORE_COLS], F32, name="result")
             for b in range(X_UNITS):
                 tiles = slice(b * UNIT_TILES, (b + 1) * UNIT_TILES)
-                unit_result = result[:, tiles, part * UNIT : (part + 1) * UNIT]
+                result = result_pool.tile([P, UNIT_TILES, UNIT], F32)
                 if n < ROTATED_UNITS:
-                    rotate(banks[b], tiles, unit_result)
+                    rotate(banks[b], tiles, result[:])
                 else:
-                    interleave(banks[b], unit_result)
-                if part == STORE_UNITS - 1:
-                    nc.sync.dma_start(out=store_targets[n // STORE_UNITS][:, tiles, :], in_=result[:, tiles, :])
+                    interleave(banks[b], result[:])
+                nc.sync.dma_start(out=unit_targets[n][:, tiles, :], in_=result[:])

@@ -77,15 +77,14 @@ def tile_mha_pa_kernel(tc, x, freqs_cos, freqs_sin, wqkv, out_0, out_1, out_2):
         ident = const.tile([P, P], F32)
         make_identity(nc, ident[:])
 
-        first_table = const.tile([P, TOKEN_TILES, UNIT_HEADS, PAIRS, 2], F32)
-        second_table = const.tile([P, TOKEN_TILES, UNIT_HEADS, PAIRS, 2], F32)
+        factors = const.tile([P, TOKEN_TILES, UNIT_TILES, UNIT_HEADS, PAIRS, 2], F32)
         over_heads = [P, TOKEN_TILES, UNIT_HEADS, PAIRS]
         cos_heads = cos_sb[:].unsqueeze(2).to_broadcast(over_heads)
         sin_heads = sin_sb[:].unsqueeze(2).to_broadcast(over_heads)
-        nc.vector.tensor_copy(out=first_table[:, :, :, :, 0], in_=cos_heads)
-        nc.vector.tensor_copy(out=first_table[:, :, :, :, 1], in_=sin_heads)
-        nc.vector.tensor_scalar_mul(out=second_table[:, :, :, :, 0], in0=sin_heads, scalar1=-1.0)
-        nc.vector.tensor_copy(out=second_table[:, :, :, :, 1], in_=cos_heads)
+        nc.vector.tensor_copy(out=factors[:, :, 0, :, :, 0], in_=cos_heads)
+        nc.vector.tensor_copy(out=factors[:, :, 0, :, :, 1], in_=sin_heads)
+        nc.vector.tensor_scalar_mul(out=factors[:, :, 1, :, :, 0], in0=sin_heads, scalar1=-1.0)
+        nc.vector.tensor_copy(out=factors[:, :, 1, :, :, 1], in_=cos_heads)
 
         def transpose_unit(raw):
             grouped = grouped_pool.tile([P, PASSES * UNIT * PACK], BF16, align_bytes=64)
@@ -131,25 +130,17 @@ def tile_mha_pa_kernel(tc, x, freqs_cos, freqs_sin, wqkv, out_0, out_1, out_2):
             return acc
 
         def rotate(acc, tiles, rotated):
-            pair_shape = [P, UNIT_TILES, P, 2]
-            from_first = product_pool.tile(pair_shape, F32)
-            from_second = product_pool.tile(pair_shape, F32)
+            products = product_pool.tile([P, UNIT_TILES, UNIT_TILES, P, 2], F32)
             nc.vector.tensor_tensor(
-                out=from_first[:],
-                in0=acc[:, :, 0:P].unsqueeze(3).to_broadcast(pair_shape),
-                in1=first_table[:, tiles, :, :, :].rearrange("p m h i e -> p m (h i) e"),
-                op=MULT,
-            )
-            nc.vector.tensor_tensor(
-                out=from_second[:],
-                in0=acc[:, :, P:UNIT].unsqueeze(3).to_broadcast(pair_shape),
-                in1=second_table[:, tiles, :, :, :].rearrange("p m h i e -> p m (h i) e"),
+                out=products[:].rearrange("p m j r e -> p (m j r) e"),
+                in0=acc[:].rearrange("p m c -> p (m c)").unsqueeze(2).to_broadcast([P, UNIT_TILES * UNIT, 2]),
+                in1=factors[:, tiles, :, :, :, :].rearrange("p m j h i e -> p (m j h i) e"),
                 op=MULT,
             )
             nc.gpsimd.tensor_tensor(
                 out=rotated,
-                in0=from_first[:].rearrange("p m r e -> p m (r e)"),
-                in1=from_second[:].rearrange("p m r e -> p m (r e)"),
+                in0=products[:, :, 0, :, :].rearrange("p m r e -> p m (r e)"),
+                in1=products[:, :, 1, :, :].rearrange("p m r e -> p m (r e)"),
                 op=ADD,
             )
 

from contextlib import ExitStack

import concourse.mybir as mybir
from concourse.masks import make_identity

F32 = mybir.dt.float32
BF16 = mybir.dt.bfloat16
U32 = mybir.dt.uint32
U8 = mybir.dt.uint8
FP8X4 = mybir.dt.float8_e4m3fn_x4
MULT = mybir.AluOpType.mult
ADD = mybir.AluOpType.add

P = 128
S = 512
D = 2048
Q_DIM = 2048
KV_DIM = 512
HEAD_DIM = 128
PAIRS = HEAD_DIM // 2

PACK = 4
K_PASS = P * PACK
PASSES = D // K_PASS
WORD_HALVES = 2
UNIT = 256
UNIT_TILES = UNIT // P
X_UNITS = S // UNIT
W_UNITS = (Q_DIM + 2 * KV_DIM) // UNIT
ROTATED_UNITS = (Q_DIM + KV_DIM) // UNIT
UNIT_HEADS = UNIT // HEAD_DIM
TOKEN_TILES = S // P
LOADS_AHEAD = 6

FLOPS = 2 * S * (Q_DIM + 2 * KV_DIM) * D


def tile_mha_pa_kernel(tc, x, freqs_cos, freqs_sin, wqkv, out_0, out_1, out_2):
    nc = tc.nc

    x_units = x.rearrange("(p n j) k -> n p j k", n=X_UNITS, j=UNIT_TILES)
    cos_rows = freqs_cos.rearrange("(p m) i -> p m i", m=TOKEN_TILES)
    sin_rows = freqs_sin.rearrange("(p m) i -> p m i", m=TOKEN_TILES)
    w_units = wqkv.rearrange("(n p j) k -> n p j k", p=P, j=UNIT_TILES)
    q_rows = out_0.rearrange("(p m) h d -> p m (h d)", m=TOKEN_TILES)
    k_rows = out_1.rearrange("(p m) h d -> p m (h d)", m=TOKEN_TILES)
    v_rows = out_2.rearrange("(p m) h d -> p m (h d)", m=TOKEN_TILES)
    unit_targets = [
        rows[:, :, c : c + UNIT]
        for rows, width in ((q_rows, Q_DIM), (k_rows, KV_DIM), (v_rows, KV_DIM))
        for c in range(0, width, UNIT)
    ]

    with ExitStack() as ctx:
        const = ctx.enter_context(tc.tile_pool(name="const", bufs=1))
        raw_pool = ctx.enter_context(tc.tile_pool(name="raw", bufs=1))
        grouped_pool = ctx.enter_context(tc.tile_pool(name="grouped", bufs=3))
        w_mx_pool = ctx.enter_context(tc.tile_pool(name="w_mx", bufs=3))
        product_pool = ctx.enter_context(tc.tile_pool(name="product", bufs=4))
        result_pool = ctx.enter_context(tc.tile_pool(name="result", bufs=8))
        flipped_pool = ctx.enter_context(tc.psum_pool(name="flipped", bufs=PASSES))
        acc_pool = ctx.enter_context(tc.psum_pool(name="acc", bufs=2 * X_UNITS))
        ctx.enter_context(tc.manual_schedule())

        def load_unit(rows, name):
            raw = raw_pool.tile([P, UNIT_TILES, D], BF16, name=name)
            nc.sync.dma_start(out=raw[:], in_=rows)
            return raw

        cos_sb = const.tile([P, TOKEN_TILES, PAIRS], BF16)
        sin_sb = const.tile([P, TOKEN_TILES, PAIRS], BF16)
        nc.scalar.dma_start(out=cos_sb[:], in_=cos_rows)
        nc.scalar.dma_start(out=sin_sb[:], in_=sin_rows)
        x_raw = [load_unit(x_units[n, :, :, :], "x_raw%d" % n) for n in range(X_UNITS)]
        w_raw = [load_unit(w_units[n, :, :, :], "w_raw%d" % n) for n in range(LOADS_AHEAD)]

        ident = const.tile([P, P], F32)
        make_identity(nc, ident[:])

        factors = const.tile([P, TOKEN_TILES, UNIT_TILES, UNIT_HEADS, PAIRS, 2], F32)
        over_heads = [P, TOKEN_TILES, UNIT_HEADS, PAIRS]
        cos_heads = cos_sb[:].unsqueeze(2).to_broadcast(over_heads)
        sin_heads = sin_sb[:].unsqueeze(2).to_broadcast(over_heads)
        nc.vector.tensor_copy(out=factors[:, :, 0, :, :, 0], in_=cos_heads)
        nc.vector.tensor_copy(out=factors[:, :, 0, :, :, 1], in_=sin_heads)
        nc.vector.tensor_scalar_mul(out=factors[:, :, 1, :, :, 0], in0=sin_heads, scalar1=-1.0)
        nc.vector.tensor_copy(out=factors[:, :, 1, :, :, 1], in_=cos_heads)

        def transpose_unit(raw):
            grouped = grouped_pool.tile([P, PASSES * UNIT * PACK], BF16, align_bytes=64)
            grouped_words = grouped[:].bitcast(F32).rearrange(
                "p (g j r u) -> p g j r u", g=PASSES, j=UNIT_TILES, u=WORD_HALVES
            )
            for g in range(PASSES):
                flipped = flipped_pool.tile([P, UNIT_TILES, WORD_HALVES, P], F32)
                for j in range(UNIT_TILES):
                    raw_words = raw[:, j, :].bitcast(F32)
                    for u in range(WORD_HALVES):
                        first = (WORD_HALVES * g + u) * P
                        nc.tensor.transpose(flipped[:, j, u, :], raw_words[:, first : first + P], ident[:])
                nc.scalar.copy(out=grouped_words[:, g, :, :, :], in_=flipped[:].rearrange("p j u r -> p j r u"))
            return grouped

        def quantise_unit(grouped, pool, name):
            codes = pool.tile([P, PASSES, UNIT], U32, name=name + "_codes", align_bytes=64)
            scales = pool.tile([P, PASSES, UNIT], U8, name=name + "_scales", align_bytes=64)
            nc.vector.quantize_mx(
                out=codes[:].rearrange("p g c -> p (g c)").bitcast(FP8X4),
                scales=scales[:].rearrange("p g c -> p (g c)"),
                in_=grouped[:],
            )
            return codes, scales

        def multiply(x_unit, w_unit):
            x_codes, x_scales = x_unit
            w_codes, w_scales = w_unit
            acc = acc_pool.tile([P, UNIT_TILES, UNIT], F32)
            for j in range(UNIT_TILES):
                tokens = slice(j * P, (j + 1) * P)
                for g in range(PASSES):
                    nc.tensor.matmul_mx(
                        out=acc[:, j, :],
                        lhsT=x_codes[:, g, tokens].bitcast(FP8X4),
                        lhsT_scale=x_scales[:, g, tokens],
                        rhs=w_codes[:, g, :].bitcast(FP8X4),
                        rhs_scale=w_scales[:, g, :],
                        start=(g == 0),
                        stop=(g == PASSES - 1),
                    )
            return acc

        def rotate(acc, tiles, rotated):
            products = product_pool.tile([P, UNIT_TILES, UNIT_TILES, P, 2], F32)
            nc.vector.tensor_tensor(
                out=products[:].rearrange("p m j r e -> p (m j r) e"),
                in0=acc[:].rearrange("p m c -> p (m c)").unsqueeze(2).to_broadcast([P, UNIT_TILES * UNIT, 2]),
                in1=factors[:, tiles, :, :, :, :].rearrange("p m j h i e -> p (m j h i) e"),
                op=MULT,
            )
            nc.gpsimd.tensor_tensor(
                out=rotated,
                in0=products[:, :, 0, :, :].rearrange("p m r e -> p m (r e)"),
                in1=products[:, :, 1, :, :].rearrange("p m r e -> p m (r e)"),
                op=ADD,
            )

        def interleave(acc, plain):
            nc.scalar.copy(
                out=plain.rearrange("p m (r j) -> p m r j", j=UNIT_TILES),
                in_=acc[:].rearrange("p m (j r) -> p m r j", j=UNIT_TILES),
            )

        x_grouped = [transpose_unit(x_raw[n]) for n in range(X_UNITS)]
        x_mx = [quantise_unit(x_grouped[n], const, "x%d" % n) for n in range(X_UNITS)]
        w_mx = quantise_unit(transpose_unit(w_raw[0]), w_mx_pool, "w")

        for n in range(W_UNITS):
            if n + LOADS_AHEAD < W_UNITS:
                w_raw.append(load_unit(w_units[n + LOADS_AHEAD, :, :, :], "w_raw%d" % (n + LOADS_AHEAD)))
            following = n + 1 < W_UNITS
            if following:
                w_grouped = transpose_unit(w_raw[n + 1])
            banks = [multiply(x_mx[b], w_mx) for b in range(X_UNITS)]
            if following:
                w_mx = quantise_unit(w_grouped, w_mx_pool, "w")

            for b in range(X_UNITS):
                tiles = slice(b * UNIT_TILES, (b + 1) * UNIT_TILES)
                result = result_pool.tile([P, UNIT_TILES, UNIT], F32)
                if n < ROTATED_UNITS:
                    rotate(banks[b], tiles, result[:])
                else:
                    interleave(banks[b], result[:])
                nc.sync.dma_start(out=unit_targets[n][:, tiles, :], in_=result[:])
